import numpy as np
import ml_dtypes


def mxq(x, axis, fmt="e4m3"):
    dtype, down = {"e4m3": (ml_dtypes.float8_e4m3fn, 7), "e5m2": (ml_dtypes.float8_e5m2, 14)}[fmt]
    v = np.moveaxis(np.asarray(x, np.float32).astype(ml_dtypes.bfloat16).astype(np.float64), axis, -1)
    blocks = v.reshape(v.shape[:-1] + (-1, 32))
    amax = np.abs(blocks).max(-1, keepdims=True)
    byte = np.maximum(np.where(amax > 0, np.frexp(amax)[1] - 1 + 127, 0) - down, 1)
    scale = np.exp2(byte - 127.0)
    codes = (blocks / scale).astype(np.float32).astype(dtype).astype(np.float64)
    return np.moveaxis((codes * scale).reshape(v.shape), -1, axis)


WIDE = False


def mx_kscale(k):
    if not WIDE:
        return np.ones(k)
    levels = np.array([10, -10, 5, -5, 0])
    a = np.random.permutation(np.resize(levels, k // 512 * 4)).reshape(k // 512, 4)
    idx = np.arange(k)
    return np.exp2(a[idx // 512, idx % 128 // 32])


BF16 = ml_dtypes.bfloat16


def bf(x):
    return np.asarray(x, np.float32).astype(BF16)


def f64(x):
    return np.asarray(x).astype(np.float64)


E2M1 = np.array([0.0, 0.5, 1.0, 1.5, 2.0, 3.0, 4.0, 6.0, -0.0, -0.5, -1.0, -1.5, -2.0, -3.0, -4.0, -6.0])


def pack_weight(w, fmt):
    k, n = w.shape
    w = f64(bf(w)).reshape(k // 32, 32, n)
    amax = np.abs(w).max(1)
    if fmt == "e4m3":
        byte = np.frexp(amax)[1] - 1 + 127 - 7
    else:
        mant, ex = np.frexp(amax / 6.0)
        byte = np.where(mant > 0.5, ex, ex - 1) + 127
    byte = np.clip(np.where(amax > 0, byte, 1), 1, 254)
    scaled = (w * np.exp2(127.0 - byte)[:, None, :]).reshape(k, n).astype(np.float32)
    by_word = np.ascontiguousarray(scaled.reshape(k // 512, 128, 4, n).transpose(0, 1, 3, 2))
    if fmt == "e4m3":
        words = by_word.astype(ml_dtypes.float8_e4m3fn).view(np.uint8)
    else:
        c = by_word.astype(ml_dtypes.float4_e2m1fn).view(np.uint8) & 0xF
        words = c[..., 0::2] | (c[..., 1::2] << 4)
    return np.ascontiguousarray(words), np.ascontiguousarray(byte.astype(np.uint8).reshape(k // 512, 16, n))


def unpack_weight(words, scales, fmt):
    g, p, n, _ = words.shape
    if fmt == "e4m3":
        vals = np.ascontiguousarray(words).view(ml_dtypes.float8_e4m3fn).astype(np.float64)
    else:
        nib = np.empty((g, p, n, 4), np.uint8)
        nib[..., 0::2] = words & 0xF
        nib[..., 1::2] = words >> 4
        vals = E2M1[nib]
    vals = vals * np.repeat(np.exp2(scales.astype(np.float64) - 127.0), 8, axis=1)[..., None]
    return vals.transpose(0, 1, 3, 2).reshape(g * 512, n)

def pack4(w):
    words, scales = pack_weight(w, "e2m1")
    return words.reshape(words.shape[0], 128, -1), scales


def unpack4(words, scales):
    return unpack_weight(words.reshape(words.shape[0], 128, -1, 2), scales, "e2m1")


B, S, DIM, H, NKV, HD, GS = 1, 128, 8192, 16, 4, 128, 128
QS = H * HD
KVS = NKV * HD
HALF = HD // 2
ROPE_BASE = 10000.0
RMS_EPS = 1.1920929e-07


def rms_norm(v):
    return v / np.sqrt(np.mean(v * v, axis=-1, keepdims=True) + RMS_EPS)


def rope_cos_sin():
    inv_freq = 1.0 / ROPE_BASE ** (np.arange(0, HD, 2) / HD)
    freqs = np.outer(np.arange(S), inv_freq)
    return np.cos(freqs)[None, :, None, :], np.sin(freqs)[None, :, None, :]


def apply_rotary_emb(u, cos, sin):
    u1, u2 = u[..., :HALF], u[..., HALF:]
    return np.concatenate((u1 * cos + u2 * sin, u1 * -sin + u2 * cos), axis=-1)


def setup_inputs():
    s = mx_kscale(DIM)
    x = bf(np.random.standard_normal((B, S, DIM)) * s)
    w = np.random.standard_normal((QS + 2 * KVS, DIM)) * 0.66 / np.sqrt(DIM) / s[None, :]
    words, scales = pack4(np.ascontiguousarray(w.T))
    q_gain = bf(1.0 + 0.1 * np.random.standard_normal(H))
    return {"x": x,
            "w_qkv_tern_words": words,
            "w_qkv_tern_scales": scales,
            "q_gain": q_gain}


def reference(x, w_qkv_tern_words, w_qkv_tern_scales, q_gain):
    qkv = mxq(f64(x), 2, "e4m3") @ unpack4(w_qkv_tern_words, w_qkv_tern_scales)
    q = qkv[..., :QS].reshape(B, S, H, HD)
    k = qkv[..., QS:QS + KVS].reshape(B, S, NKV, HD)
    v = qkv[..., QS + KVS:].reshape(B, S, NKV, HD)
    q, k = rms_norm(q), rms_norm(k)
    cos, sin = rope_cos_sin()
    q = apply_rotary_emb(q, cos, sin)
    k = apply_rotary_emb(k, cos, sin)
    q = q * f64(q_gain)[None, None, :, None]
    return q, k, v

@@ -1,0 +1,263 @@
+import math
+from contextlib import ExitStack
+
+import concourse.mybir as mybir
+from concourse.masks import make_identity
+
+F32 = mybir.dt.float32
+BF16 = mybir.dt.bfloat16
+I32 = mybir.dt.int32
+U32 = mybir.dt.uint32
+U8 = mybir.dt.uint8
+FP8X4 = mybir.dt.float8_e4m3fn_x4
+FP4X4 = mybir.dt.float4_e2m1fn_x4
+ALU = mybir.AluOpType
+ACT = mybir.ActivationFunctionType
+
+P = 128
+PACK = 4
+K_GROUP = P * PACK
+DIM = 8192
+GROUPS = DIM // K_GROUP
+HEAD = 128
+HALF = HEAD // 2
+BANK = 512
+HEADS_PER_BANK = BANK // HEAD
+Q_COLS = 16 * HEAD
+KV_COLS = 4 * HEAD
+N_ALL = Q_COLS + 2 * KV_COLS
+Q_BANKS = Q_COLS // BANK
+K_BANK = Q_BANKS
+V_BANK = Q_BANKS + 1
+N_BANKS = N_ALL // BANK
+ROPE_BASE = 10000.0
+RMS_EPS = 1.1920929e-07
+
+X_CHUNK_GROUPS = 4
+SCALE_RUNS = 2
+GROUPS_PER_SCALE_DMA = 4
+
+ROUND_MAGIC = 12582912.0
+TWO_PI_HIGH = 6.28125
+TWO_PI_MID = 0.0019350051879882812
+TWO_PI_LOW = 2.0 * math.pi - TWO_PI_HIGH - TWO_PI_MID
+
+FLOPS = 2 * P * DIM * N_ALL
+
+
+def load_weight_scales(nc, planes_i32, scales_by_row, first_group, n_groups):
+    for first in range(first_group, first_group + n_groups, GROUPS_PER_SCALE_DMA):
+        some = slice(first, first + GROUPS_PER_SCALE_DMA)
+        for quadrant in range(2):
+            for row in range(4):
+                nc.sync.dma_start(
+                    out=planes_i32[32 * quadrant + row : P : 64, some, :],
+                    in_=scales_by_row[row, quadrant:4:2, some, :],
+                )
+
+
+def load_weight_words(nc, w_words, words, group, first_col, n_cols):
+    some = slice(2 * first_col, 2 * (first_col + n_cols))
+    nc.sync.dma_start(
+        out=w_words[:, group, some].bitcast(I32), in_=words[group, :, some].bitcast(I32)
+    )
+
+
+def build_rotation_table(nc, pool):
+    token_i = pool.tile([P, 1], I32)
+    nc.gpsimd.iota(token_i[:], pattern=[[0, 1]], base=0, channel_multiplier=1)
+    token = pool.tile([P, 1], F32)
+    nc.vector.tensor_copy(out=token[:], in_=token_i[:])
+
+    inv_freq = pool.tile([P, HALF], F32)
+    nc.vector.memset(inv_freq[:], 1.0)
+    for step in (1, 2, 4, 8, 16, 32):
+        bit_set = inv_freq[:].rearrange("p (a b c) -> p a b c", b=2, c=step)[:, :, 1, :]
+        nc.vector.tensor_scalar_mul(out=bit_set, in0=bit_set, scalar1=ROPE_BASE ** (-step / HALF))
+
+    angle = pool.tile([P, 2, HALF], F32)
+    nc.vector.tensor_scalar_mul(out=angle[:, 0, :], in0=inv_freq[:], scalar1=token[:, 0:1])
+    nc.vector.tensor_scalar(
+        out=angle[:, 1, :],
+        in0=inv_freq[:],
+        scalar1=token[:, 0:1],
+        scalar2=math.pi / 2.0,
+        op0=ALU.mult,
+        op1=ALU.add,
+    )
+    flat_angle = angle[:].rearrange("p a j -> p (a j)")
+    turns = pool.tile([P, 2 * HALF], F32)
+    nc.vector.tensor_scalar(
+        out=turns[:],
+        in0=flat_angle,
+        scalar1=1.0 / (2.0 * math.pi),
+        scalar2=ROUND_MAGIC,
+        op0=ALU.mult,
+        op1=ALU.add,
+    )
+    nc.vector.tensor_single_scalar(out=turns[:], in_=turns[:], scalar=ROUND_MAGIC, op=ALU.subtract)
+    for part in (TWO_PI_HIGH, TWO_PI_MID, TWO_PI_LOW):
+        nc.vector.scalar_tensor_tensor(
+            out=flat_angle, in0=turns[:], scalar=-part, in1=flat_angle, op0=ALU.mult, op1=ALU.add
+        )
+    table = pool.tile([P, 3, HALF], F32)
+    nc.scalar.activation(out=table[:, 0:2, :], in_=angle[:], func=ACT.Sin)
+    nc.vector.tensor_scalar_mul(out=table[:, 2, :], in0=table[:, 0, :], scalar1=-1.0)
+    return table
+
+
+def tile_causalselfattention_pa_k_kernel(
+    tc, x, w_qkv_tern_words, w_qkv_tern_scales, q_gain, out_0, out_1, out_2
+):
+    nc = tc.nc
+    x_rows = x.flatten_outer_dims()
+    q_rows = out_0.rearrange("b s h d -> (b s) (h d)")
+    k_rows = out_1.rearrange("b s h d -> (b s) (h d)")
+    v_rows = out_2.rearrange("b s h d -> (b s) (h d)")
+    scales_by_row = w_qkv_tern_scales.bitcast(I32).rearrange(
+        "g (quadrant row) n -> row quadrant g n", row=4
+    )
+
+    with ExitStack() as ctx:
+        ctx.enter_context(tc.manual_schedule())
+        keep = ctx.enter_context(tc.tile_pool(name="keep", bufs=1))
+        work = ctx.enter_context(tc.tile_pool(name="work", bufs=2))
+        psum_x = ctx.enter_context(tc.psum_pool(name="psum_x", bufs=2))
+        psum_acc = ctx.enter_context(tc.psum_pool(name="psum_acc", bufs=1))
+
+        x_sb = keep.tile([P, DIM], BF16)
+        x_grouped = keep.tile([P, GROUPS, P * PACK], BF16, align_bytes=64)
+        x_codes = keep.tile([P, GROUPS, P], U32, align_bytes=64)
+        x_planes = keep.tile([P, GROUPS, P], U8, align_bytes=64)
+        w_words = keep.tile([P, GROUPS, 2 * N_ALL], U8, align_bytes=64)
+        w_planes = keep.tile([P, GROUPS, N_ALL], U8, align_bytes=64)
+        gain_bf = keep.tile([P, Q_COLS // HEAD], BF16)
+        gain = keep.tile([P, Q_COLS // HEAD], F32)
+        eps = keep.tile([P, 1], F32)
+        identity = keep.tile([P, P], F32)
+        staged = keep.tile([P, N_ALL], F32)
+        planes_i32 = w_planes[:].bitcast(I32)
+
+        make_identity(nc, identity[:])
+
+        x_chunk = X_CHUNK_GROUPS * K_GROUP
+        for first in range(0, DIM, x_chunk):
+            nc.sync.dma_start(
+                out=x_sb[:, first : first + x_chunk], in_=x_rows[:, first : first + x_chunk]
+            )
+        nc.sync.dma_start(out=gain_bf[:], in_=q_gain.partition_broadcast(P))
+        run_groups = GROUPS // SCALE_RUNS
+        for first_group in range(0, GROUPS, run_groups):
+            nc.vector.memset(planes_i32[:, first_group : first_group + run_groups, :], 0)
+            load_weight_scales(nc, planes_i32, scales_by_row, first_group, run_groups)
+            for g in range(first_group, first_group + run_groups):
+                load_weight_words(nc, w_words, w_qkv_tern_words, g, 0, Q_COLS)
+        for g in range(GROUPS):
+            load_weight_words(nc, w_words, w_qkv_tern_words, g, Q_COLS, 2 * KV_COLS)
+
+        x_words = x_sb[:].bitcast(F32)
+        grouped_words = x_grouped[:].bitcast(F32).rearrange("p g (s u) -> p g s u", u=2)
+        words_per_group = K_GROUP // 2
+        for first_group in range(0, GROUPS, X_CHUNK_GROUPS):
+            for pair in range(first_group, first_group + X_CHUNK_GROUPS, 2):
+                x_t = psum_x.tile([P, 2, 2, P], F32)
+                for i in range(2):
+                    start_word = (pair + i) * words_per_group
+                    for u in range(2):
+                        nc.tensor.transpose(
+                            x_t[:, i, u, :],
+                            x_words[:, start_word + u : start_word + words_per_group : 2],
+                            identity[:],
+                        )
+                nc.scalar.copy(
+                    out=grouped_words[:, pair : pair + 2, :, :],
+                    in_=x_t[:].rearrange("p i u s -> p i s u"),
+                )
+            some = slice(first_group, first_group + X_CHUNK_GROUPS)
+            nc.vector.quantize_mx(
+                out=x_codes[:, some, :].rearrange("p g s -> p (g s)").bitcast(FP8X4),
+                scales=x_planes[:, some, :].rearrange("p g s -> p (g s)"),
+                in_=x_grouped[:, some, :].rearrange("p g c -> p (g c)"),
+            )
+
+        table = build_rotation_table(nc, keep)
+        sin_j = table[:, 0, :].unsqueeze(1).to_broadcast([P, HEADS_PER_BANK, HALF])
+        cos_j = table[:, 1, :].unsqueeze(1).unsqueeze(1).to_broadcast([P, HEADS_PER_BANK, 2, HALF])
+        minus_sin_j = table[:, 2, :].unsqueeze(1).to_broadcast([P, HEADS_PER_BANK, HALF])
+        nc.vector.tensor_copy(out=gain[:], in_=gain_bf[:])
+        nc.vector.memset(eps[:], RMS_EPS)
+
+        acc = [psum_acc.tile([P, BANK], F32, name="acc%d" % b) for b in range(N_BANKS)]
+        root = [keep.tile([P, HEADS_PER_BANK], F32, name="root%d" % b) for b in range(K_BANK + 1)]
+        factor = [keep.tile([P, HEADS_PER_BANK], F32, name="factor%d" % b) for b in range(K_BANK + 1)]
+
+        def multiply(g, b):
+            nc.tensor.matmul_mx(
+                out=acc[b][:],
+                lhsT=x_codes[:, g, :].bitcast(FP8X4),
+                lhsT_scale=x_planes[:, g, :],
+                rhs=w_words[:, g, 2 * BANK * b : 2 * BANK * (b + 1)].bitcast(FP4X4),
+                rhs_scale=w_planes[:, g, BANK * b : BANK * (b + 1)],
+                start=(g == 0),
+                stop=(g == GROUPS - 1),
+            )
+
+        def root_mean_square(b):
+            squares = work.tile([P, BANK], F32)
+            sum_sq = work.tile([P, HEADS_PER_BANK], F32)
+            for h in range(HEADS_PER_BANK):
+                cols = slice(h * HEAD, (h + 1) * HEAD)
+                nc.scalar.activation(
+                    out=squares[:, cols],
+                    in_=acc[b][:, cols],
+                    func=ACT.Square,
+                    accum_out=sum_sq[:, h : h + 1],
+                )
+            nc.scalar.activation(
+                out=root[b][:], in_=sum_sq[:], func=ACT.Sqrt, scale=1.0 / HEAD, bias=eps[:, 0:1]
+            )
+
+        def rotate(b, adder):
+            nc.vector.reciprocal(out=factor[b][:], in_=root[b][:])
+            if b < Q_BANKS:
+                heads = slice(b * HEADS_PER_BANK, (b + 1) * HEADS_PER_BANK)
+                nc.vector.tensor_mul(out=factor[b][:], in0=factor[b][:], in1=gain[:, heads])
+            u = acc[b][:].rearrange("p (h two j) -> p h two j", two=2, j=HALF)
+            same = staged[:, BANK * b : BANK * (b + 1)]
+            cross = work.tile([P, HEADS_PER_BANK, 2, HALF], F32)
+            nc.vector.tensor_mul(
+                out=same.rearrange("p (h two j) -> p h two j", two=2, j=HALF), in0=u, in1=cos_j
+            )
+            nc.vector.tensor_mul(out=cross[:, :, 0, :], in0=u[:, :, 1, :], in1=sin_j)
+            nc.vector.tensor_mul(out=cross[:, :, 1, :], in0=u[:, :, 0, :], in1=minus_sin_j)
+            adder.tensor_add(out=same, in0=same, in1=cross[:].rearrange("p h two j -> p (h two j)"))
+
+        def scale_heads(b):
+            for h in range(HEADS_PER_BANK):
+                cols = slice(BANK * b + h * HEAD, BANK * b + (h + 1) * HEAD)
+                nc.scalar.activation(
+                    out=staged[:, cols], in_=staged[:, cols], func=ACT.Copy, scale=factor[b][:, h : h + 1]
+                )
+
+        for g in range(GROUPS):
+            for b in range(Q_BANKS):
+                multiply(g, b)
+        for b in range(Q_BANKS):
+            root_mean_square(b)
+        for b in range(Q_BANKS):
+            rotate(b, nc.gpsimd)
+        for b in range(Q_BANKS):
+            scale_heads(b)
+            nc.sync.dma_start(
+                out=q_rows[:, BANK * b : BANK * (b + 1)], in_=staged[:, BANK * b : BANK * (b + 1)]
+            )
+
+        for g in range(GROUPS):
+            multiply(g, K_BANK)
+            multiply(g, V_BANK)
+        root_mean_square(K_BANK)
+        nc.vector.tensor_copy(out=staged[:, BANK * V_BANK : BANK * (V_BANK + 1)], in_=acc[V_BANK][:])
+        nc.sync.dma_start(out=v_rows, in_=staged[:, BANK * V_BANK : BANK * (V_BANK + 1)])
+        rotate(K_BANK, nc.vector)
+        scale_heads(K_BANK)
+        nc.sync.dma_start(out=k_rows, in_=staged[:, BANK * K_BANK : BANK * (K_BANK + 1)])

@@ -34,8 +34,8 @@ ROPE_BASE = 10000.0
 RMS_EPS = 1.1920929e-07
 
 X_CHUNK_GROUPS = 4
-SCALE_RUNS = 2
 GROUPS_PER_SCALE_DMA = 4
+GAIN_PAD = 32
 
 ROUND_MAGIC = 12582912.0
 TWO_PI_HIGH = 6.28125
@@ -45,15 +45,11 @@ TWO_PI_LOW = 2.0 * math.pi - TWO_PI_HIGH - TWO_PI_MID
 FLOPS = 2 * P * DIM * N_ALL
 
 
-def load_weight_scales(nc, planes_i32, scales_by_row, first_group, n_groups):
-    for first in range(first_group, first_group + n_groups, GROUPS_PER_SCALE_DMA):
-        some = slice(first, first + GROUPS_PER_SCALE_DMA)
-        for quadrant in range(2):
-            for row in range(4):
-                nc.sync.dma_start(
-                    out=planes_i32[32 * quadrant + row : P : 64, some, :],
-                    in_=scales_by_row[row, quadrant:4:2, some, :],
-                )
+def load_weight_scales(queue, planes, scales, word, first_group):
+    some = slice(first_group, first_group + GROUPS_PER_SCALE_DMA)
+    by_row = scales.bitcast(word).rearrange("g (quadrant row) n -> row quadrant g n", row=4)
+    for row in range(4):
+        queue.dma_start(out=planes.bitcast(word)[row:P:32, some, :], in_=by_row[row, :, some, :])
 
 
 def load_weight_words(nc, w_words, words, group, first_col, n_cols):
@@ -114,9 +110,6 @@ def tile_causalselfattention_pa_k_kernel(
     q_rows = out_0.rearrange("b s h d -> (b s) (h d)")
     k_rows = out_1.rearrange("b s h d -> (b s) (h d)")
     v_rows = out_2.rearrange("b s h d -> (b s) (h d)")
-    scales_by_row = w_qkv_tern_scales.bitcast(I32).rearrange(
-        "g (quadrant row) n -> row quadrant g n", row=4
-    )
 
     with ExitStack() as ctx:
         ctx.enter_context(tc.manual_schedule())
@@ -131,27 +124,30 @@ def tile_causalselfattention_pa_k_kernel(
         x_planes = keep.tile([P, GROUPS, P], U8, align_bytes=64)
         w_words = keep.tile([P, GROUPS, 2 * N_ALL], U8, align_bytes=64)
         w_planes = keep.tile([P, GROUPS, N_ALL], U8, align_bytes=64)
-        gain_bf = keep.tile([P, Q_COLS // HEAD], BF16)
+        gain_row = keep.tile([P, GAIN_PAD], BF16)
+        ones = keep.tile([P, P], BF16)
         gain = keep.tile([P, Q_COLS // HEAD], F32)
         eps = keep.tile([P, 1], F32)
         identity = keep.tile([P, P], F32)
         staged = keep.tile([P, N_ALL], F32)
-        planes_i32 = w_planes[:].bitcast(I32)
 
         make_identity(nc, identity[:])
+        nc.vector.memset(gain_row[:], 0.0)
+        nc.vector.memset(ones[:], 1.0)
 
+        for first in range(0, GROUPS, GROUPS_PER_SCALE_DMA):
+            nc.vector.memset(w_planes[:].bitcast(I32)[:, first : first + GROUPS_PER_SCALE_DMA, :], 0)
         x_chunk = X_CHUNK_GROUPS * K_GROUP
         for first in range(0, DIM, x_chunk):
             nc.sync.dma_start(
                 out=x_sb[:, first : first + x_chunk], in_=x_rows[:, first : first + x_chunk]
             )
-        nc.sync.dma_start(out=gain_bf[:], in_=q_gain.partition_broadcast(P))
-        run_groups = GROUPS // SCALE_RUNS
-        for first_group in range(0, GROUPS, run_groups):
-            nc.vector.memset(planes_i32[:, first_group : first_group + run_groups, :], 0)
-            load_weight_scales(nc, planes_i32, scales_by_row, first_group, run_groups)
-            for g in range(first_group, first_group + run_groups):
-                load_weight_words(nc, w_words, w_qkv_tern_words, g, 0, Q_COLS)
+        load_weight_scales(nc.sync, w_planes[:], w_qkv_tern_scales, I32, 0)
+        for first in range(GROUPS_PER_SCALE_DMA, GROUPS, GROUPS_PER_SCALE_DMA):
+            load_weight_scales(nc.gpsimd, w_planes[:], w_qkv_tern_scales, F32, first)
+        nc.sync.dma_start(out=gain_row[0:1, 0 : Q_COLS // HEAD], in_=q_gain.unsqueeze(0))
+        for g in range(GROUPS):
+            load_weight_words(nc, w_words, w_qkv_tern_words, g, 0, Q_COLS)
         for g in range(GROUPS):
             load_weight_words(nc, w_words, w_qkv_tern_words, g, Q_COLS, 2 * KV_COLS)
 
@@ -184,7 +180,9 @@ def tile_causalselfattention_pa_k_kernel(
         sin_j = table[:, 0, :].unsqueeze(1).to_broadcast([P, HEADS_PER_BANK, HALF])
         cos_j = table[:, 1, :].unsqueeze(1).unsqueeze(1).to_broadcast([P, HEADS_PER_BANK, 2, HALF])
         minus_sin_j = table[:, 2, :].unsqueeze(1).to_broadcast([P, HEADS_PER_BANK, HALF])
-        nc.vector.tensor_copy(out=gain[:], in_=gain_bf[:])
+        gain_ps = psum_x.tile([P, GAIN_PAD], F32, tag="x_t")
+        nc.tensor.matmul(out=gain_ps[:], lhsT=ones[:], rhs=gain_row[:], start=True, stop=True)
+        nc.vector.tensor_copy(out=gain[:], in_=gain_ps[:, 0 : Q_COLS // HEAD])
         nc.vector.memset(eps[:], RMS_EPS)
 
         acc = [psum_acc.tile([P, BANK], F32, name="acc%d" % b) for b in range(N_BANKS)]

@@ -34,7 +34,8 @@ ROPE_BASE = 10000.0
 RMS_EPS = 1.1920929e-07
 
 X_CHUNK_GROUPS = 4
-GROUPS_PER_SCALE_DMA = 4
+SCALE_CHUNK = 4
+GROUPS_PER_KV_LOAD = 4
 GAIN_PAD = 32
 
 ROUND_MAGIC = 12582912.0
@@ -46,16 +47,18 @@ FLOPS = 2 * P * DIM * N_ALL
 
 
 def load_weight_scales(queue, planes, scales, word, first_group):
-    some = slice(first_group, first_group + GROUPS_PER_SCALE_DMA)
+    some = slice(first_group, first_group + SCALE_CHUNK)
     by_row = scales.bitcast(word).rearrange("g (quadrant row) n -> row quadrant g n", row=4)
     for row in range(4):
-        queue.dma_start(out=planes.bitcast(word)[row:P:32, some, :], in_=by_row[row, :, some, :])
+        queue.dma_start(out=planes.bitcast(word)[row:P:32, :, :], in_=by_row[row, :, some, :])
 
 
-def load_weight_words(nc, w_words, words, group, first_col, n_cols):
-    some = slice(2 * first_col, 2 * (first_col + n_cols))
+def load_weight_words(nc, block_words, words, first_group, n_groups, first_col):
+    groups = slice(first_group, first_group + n_groups)
+    some = slice(2 * first_col, 2 * first_col + block_words.shape[2])
     nc.sync.dma_start(
-        out=w_words[:, group, some].bitcast(I32), in_=words[group, :, some].bitcast(I32)
+        out=block_words[:, groups, :].bitcast(I32),
+        in_=words[groups, :, some].bitcast(I32).rearrange("g p c -> p g c"),
     )
 
 
@@ -122,8 +125,13 @@ def tile_causalselfattention_pa_k_kernel(
         x_grouped = keep.tile([P, GROUPS, P * PACK], BF16, align_bytes=64)
         x_codes = keep.tile([P, GROUPS, P], U32, align_bytes=64)
         x_planes = keep.tile([P, GROUPS, P], U8, align_bytes=64)
-        w_words = keep.tile([P, GROUPS, 2 * N_ALL], U8, align_bytes=64)
-        w_planes = keep.tile([P, GROUPS, N_ALL], U8, align_bytes=64)
+        q_words = keep.tile([P, GROUPS, 2 * Q_COLS], U8, align_bytes=64)
+        k_words = keep.tile([P, GROUPS, 2 * KV_COLS], U8, align_bytes=64)
+        v_words = keep.tile([P, GROUPS, 2 * KV_COLS], U8, align_bytes=64)
+        w_planes = [
+            keep.tile([P, SCALE_CHUNK, N_ALL], U8, align_bytes=64, name="w_planes%d" % c)
+            for c in range(GROUPS // SCALE_CHUNK)
+        ]
         gain_row = keep.tile([P, GAIN_PAD], BF16)
         ones = keep.tile([P, P], BF16)
         gain = keep.tile([P, Q_COLS // HEAD], F32)
@@ -135,21 +143,23 @@ def tile_causalselfattention_pa_k_kernel(
         nc.vector.memset(gain_row[:], 0.0)
         nc.vector.memset(ones[:], 1.0)
 
-        for first in range(0, GROUPS, GROUPS_PER_SCALE_DMA):
-            nc.vector.memset(w_planes[:].bitcast(I32)[:, first : first + GROUPS_PER_SCALE_DMA, :], 0)
+        for planes in w_planes:
+            nc.vector.memset(planes[:].bitcast(I32), 0)
         x_chunk = X_CHUNK_GROUPS * K_GROUP
         for first in range(0, DIM, x_chunk):
             nc.sync.dma_start(
                 out=x_sb[:, first : first + x_chunk], in_=x_rows[:, first : first + x_chunk]
             )
-        load_weight_scales(nc.sync, w_planes[:], w_qkv_tern_scales, I32, 0)
-        for first in range(GROUPS_PER_SCALE_DMA, GROUPS, GROUPS_PER_SCALE_DMA):
-            load_weight_scales(nc.gpsimd, w_planes[:], w_qkv_tern_scales, F32, first)
+        load_weight_scales(nc.sync, w_planes[0][:], w_qkv_tern_scales, I32, 0)
+        for c in range(1, GROUPS // SCALE_CHUNK):
+            load_weight_scales(nc.gpsimd, w_planes[c][:], w_qkv_tern_scales, F32, c * SCALE_CHUNK)
         nc.sync.dma_start(out=gain_row[0:1, 0 : Q_COLS // HEAD], in_=q_gain.unsqueeze(0))
         for g in range(GROUPS):
-            load_weight_words(nc, w_words, w_qkv_tern_words, g, 0, Q_COLS)
-        for g in range(GROUPS):
-            load_weight_words(nc, w_words, w_qkv_tern_words, g, Q_COLS, 2 * KV_COLS)
+            load_weight_words(nc, q_words, w_qkv_tern_words, g, 1, 0)
+        for g in range(0, GROUPS, GROUPS_PER_KV_LOAD):
+            load_weight_words(nc, k_words, w_qkv_tern_words, g, GROUPS_PER_KV_LOAD, Q_COLS)
+        for g in range(0, GROUPS, GROUPS_PER_KV_LOAD):
+            load_weight_words(nc, v_words, w_qkv_tern_words, g, GROUPS_PER_KV_LOAD, Q_COLS + KV_COLS)
 
         x_words = x_sb[:].bitcast(F32)
         grouped_words = x_grouped[:].bitcast(F32).rearrange("p g (s u) -> p g s u", u=2)
@@ -189,13 +199,13 @@ def tile_causalselfattention_pa_k_kernel(
         root = [keep.tile([P, HEADS_PER_BANK], F32, name="root%d" % b) for b in range(K_BANK + 1)]
         factor = [keep.tile([P, HEADS_PER_BANK], F32, name="factor%d" % b) for b in range(K_BANK + 1)]
 
-        def multiply(g, b):
+        def multiply(g, b, bank_words):
             nc.tensor.matmul_mx(
                 out=acc[b][:],
                 lhsT=x_codes[:, g, :].bitcast(FP8X4),
                 lhsT_scale=x_planes[:, g, :],
-                rhs=w_words[:, g, 2 * BANK * b : 2 * BANK * (b + 1)].bitcast(FP4X4),
-                rhs_scale=w_planes[:, g, BANK * b : BANK * (b + 1)],
+                rhs=bank_words.bitcast(FP4X4),
+                rhs_scale=w_planes[g // SCALE_CHUNK][:, g % SCALE_CHUNK, BANK * b : BANK * (b + 1)],
                 start=(g == 0),
                 stop=(g == GROUPS - 1),
             )
@@ -215,7 +225,7 @@ def tile_causalselfattention_pa_k_kernel(
                 out=root[b][:], in_=sum_sq[:], func=ACT.Sqrt, scale=1.0 / HEAD, bias=eps[:, 0:1]
             )
 
-        def rotate(b, adder):
+        def rotate(b):
             nc.vector.reciprocal(out=factor[b][:], in_=root[b][:])
             if b < Q_BANKS:
                 heads = slice(b * HEADS_PER_BANK, (b + 1) * HEADS_PER_BANK)
@@ -228,7 +238,7 @@ def tile_causalselfattention_pa_k_kernel(
             )
             nc.vector.tensor_mul(out=cross[:, :, 0, :], in0=u[:, :, 1, :], in1=sin_j)
             nc.vector.tensor_mul(out=cross[:, :, 1, :], in0=u[:, :, 0, :], in1=minus_sin_j)
-            adder.tensor_add(out=same, in0=same, in1=cross[:].rearrange("p h two j -> p (h two j)"))
+            nc.gpsimd.tensor_add(out=same, in0=same, in1=cross[:].rearrange("p h two j -> p (h two j)"))
 
         def scale_heads(b):
             for h in range(HEADS_PER_BANK):
@@ -237,25 +247,25 @@ def tile_causalselfattention_pa_k_kernel(
                     out=staged[:, cols], in_=staged[:, cols], func=ACT.Copy, scale=factor[b][:, h : h + 1]
                 )
 
-        for g in range(GROUPS):
-            for b in range(Q_BANKS):
-                multiply(g, b)
-        for b in range(Q_BANKS):
-            root_mean_square(b)
-        for b in range(Q_BANKS):
-            rotate(b, nc.gpsimd)
-        for b in range(Q_BANKS):
-            scale_heads(b)
-            nc.sync.dma_start(
-                out=q_rows[:, BANK * b : BANK * (b + 1)], in_=staged[:, BANK * b : BANK * (b + 1)]
-            )
+        def store(rows, b):
+            nc.sync.dma_start(out=rows, in_=staged[:, BANK * b : BANK * (b + 1)])
 
         for g in range(GROUPS):
-            multiply(g, K_BANK)
-            multiply(g, V_BANK)
-        root_mean_square(K_BANK)
+            for b in range(Q_BANKS):
+                multiply(g, b, q_words[:, g, 2 * BANK * b : 2 * BANK * (b + 1)])
+        for g in range(GROUPS):
+            multiply(g, K_BANK, k_words[:, g, :])
+        for g in range(GROUPS):
+            multiply(g, V_BANK, v_words[:, g, :])
+
+        for b in range(K_BANK + 1):
+            root_mean_square(b)
+        for b in range(K_BANK + 1):
+            rotate(b)
         nc.vector.tensor_copy(out=staged[:, BANK * V_BANK : BANK * (V_BANK + 1)], in_=acc[V_BANK][:])
-        nc.sync.dma_start(out=v_rows, in_=staged[:, BANK * V_BANK : BANK * (V_BANK + 1)])
-        rotate(K_BANK, nc.vector)
+        for b in range(Q_BANKS):
+            scale_heads(b)
+            store(q_rows[:, BANK * b : BANK * (b + 1)], b)
+        store(v_rows, V_BANK)
         scale_heads(K_BANK)
-        nc.sync.dma_start(out=k_rows, in_=staged[:, BANK * K_BANK : BANK * (K_BANK + 1)])
+        store(k_rows, K_BANK)

@@ -23,19 +23,15 @@ HEAD = 128
 HALF = HEAD // 2
 BANK = 512
 HEADS_PER_BANK = BANK // HEAD
-Q_COLS = 16 * HEAD
-KV_COLS = 4 * HEAD
-N_ALL = Q_COLS + 2 * KV_COLS
-Q_BANKS = Q_COLS // BANK
-K_BANK = Q_BANKS
-V_BANK = Q_BANKS + 1
-N_BANKS = N_ALL // BANK
+Q_HEADS = 16
+N_BANKS = 6
+V_BANK = 5
+BLOCKS = ((0, 2), (2, 2), (4, 1), (V_BANK, 1))
 ROPE_BASE = 10000.0
 RMS_EPS = 1.1920929e-07
 
 X_CHUNK_GROUPS = 4
-SCALE_CHUNK = 4
-GROUPS_PER_KV_LOAD = 4
+PASSES_PER_LOAD = 4
 GAIN_PAD = 32
 
 ROUND_MAGIC = 12582912.0
@@ -43,28 +39,28 @@ TWO_PI_HIGH = 6.28125
 TWO_PI_MID = 0.0019350051879882812
 TWO_PI_LOW = 2.0 * math.pi - TWO_PI_HIGH - TWO_PI_MID
 
-FLOPS = 2 * P * DIM * N_ALL
+FLOPS = 2 * P * DIM * N_BANKS * BANK
 
 
-def load_weight_scales(queue, planes, scales, word, first_group):
-    some = slice(first_group, first_group + SCALE_CHUNK)
+def load_block_scales(queue, planes, scales, word, first_bank, n_banks):
+    some = slice(first_bank * BANK // 4, (first_bank + n_banks) * BANK // 4)
     by_row = scales.bitcast(word).rearrange("g (quadrant row) n -> row quadrant g n", row=4)
     for row in range(4):
-        queue.dma_start(out=planes.bitcast(word)[row:P:32, :, :], in_=by_row[row, :, some, :])
+        queue.dma_start(out=planes.bitcast(word)[row:P:32, :, :], in_=by_row[row, :, :, some])
 
 
-def load_weight_words(nc, block_words, words, first_group, n_groups, first_col):
-    groups = slice(first_group, first_group + n_groups)
-    some = slice(2 * first_col, 2 * first_col + block_words.shape[2])
-    nc.sync.dma_start(
-        out=block_words[:, groups, :].bitcast(I32),
-        in_=words[groups, :, some].bitcast(I32).rearrange("g p c -> p g c"),
-    )
+def load_block_words(nc, block_words, words, first_bank, n_banks):
+    some = slice(2 * BANK * first_bank, 2 * BANK * (first_bank + n_banks))
+    groups_per_load = PASSES_PER_LOAD // n_banks
+    for first in range(0, GROUPS, groups_per_load):
+        groups = slice(first, first + groups_per_load)
+        nc.sync.dma_start(
+            out=block_words[:, groups, :].bitcast(I32),
+            in_=words[groups, :, some].bitcast(I32).rearrange("g p c -> p g c"),
+        )
 
 
-def build_rotation_table(nc, pool):
-    token_i = pool.tile([P, 1], I32)
-    nc.gpsimd.iota(token_i[:], pattern=[[0, 1]], base=0, channel_multiplier=1)
+def build_rotation_table(nc, pool, token_i):
     token = pool.tile([P, 1], F32)
     nc.vector.tensor_copy(out=token[:], in_=token_i[:])
 
@@ -113,6 +109,7 @@ def tile_causalselfattention_pa_k_kernel(
     q_rows = out_0.rearrange("b s h d -> (b s) (h d)")
     k_rows = out_1.rearrange("b s h d -> (b s) (h d)")
     v_rows = out_2.rearrange("b s h d -> (b s) (h d)")
+    block_rows = (q_rows[:, 0 : 2 * BANK], q_rows[:, 2 * BANK : 4 * BANK], k_rows, v_rows)
 
     with ExitStack() as ctx:
         ctx.enter_context(tc.manual_schedule())
@@ -125,41 +122,42 @@ def tile_causalselfattention_pa_k_kernel(
         x_grouped = keep.tile([P, GROUPS, P * PACK], BF16, align_bytes=64)
         x_codes = keep.tile([P, GROUPS, P], U32, align_bytes=64)
         x_planes = keep.tile([P, GROUPS, P], U8, align_bytes=64)
-        q_words = keep.tile([P, GROUPS, 2 * Q_COLS], U8, align_bytes=64)
-        k_words = keep.tile([P, GROUPS, 2 * KV_COLS], U8, align_bytes=64)
-        v_words = keep.tile([P, GROUPS, 2 * KV_COLS], U8, align_bytes=64)
+        w_words = [
+            keep.tile([P, GROUPS, 2 * BANK * n], U8, align_bytes=64, name="w_words%d" % first)
+            for first, n in BLOCKS
+        ]
         w_planes = [
-            keep.tile([P, SCALE_CHUNK, N_ALL], U8, align_bytes=64, name="w_planes%d" % c)
-            for c in range(GROUPS // SCALE_CHUNK)
+            keep.tile([P, GROUPS, BANK * n], U8, align_bytes=64, name="w_planes%d" % first)
+            for first, n in BLOCKS
         ]
         gain_row = keep.tile([P, GAIN_PAD], BF16)
         ones = keep.tile([P, P], BF16)
-        gain = keep.tile([P, Q_COLS // HEAD], F32)
+        gain = keep.tile([P, Q_HEADS], F32)
         eps = keep.tile([P, 1], F32)
         identity = keep.tile([P, P], F32)
-        staged = keep.tile([P, N_ALL], F32)
+        token_i = keep.tile([P, 1], I32)
+        staged = keep.tile([P, N_BANKS * BANK], F32)
 
         make_identity(nc, identity[:])
-        nc.vector.memset(gain_row[:], 0.0)
-        nc.vector.memset(ones[:], 1.0)
+        nc.gpsimd.iota(token_i[:], pattern=[[0, 1]], base=0, channel_multiplier=1)
 
         for planes in w_planes:
             nc.vector.memset(planes[:].bitcast(I32), 0)
+        nc.vector.memset(gain_row[:], 0.0)
+        nc.vector.memset(ones[:], 1.0)
         x_chunk = X_CHUNK_GROUPS * K_GROUP
         for first in range(0, DIM, x_chunk):
             nc.sync.dma_start(
                 out=x_sb[:, first : first + x_chunk], in_=x_rows[:, first : first + x_chunk]
             )
-        load_weight_scales(nc.sync, w_planes[0][:], w_qkv_tern_scales, I32, 0)
-        for c in range(1, GROUPS // SCALE_CHUNK):
-            load_weight_scales(nc.gpsimd, w_planes[c][:], w_qkv_tern_scales, F32, c * SCALE_CHUNK)
-        nc.sync.dma_start(out=gain_row[0:1, 0 : Q_COLS // HEAD], in_=q_gain.unsqueeze(0))
-        for g in range(GROUPS):
-            load_weight_words(nc, q_words, w_qkv_tern_words, g, 1, 0)
-        for g in range(0, GROUPS, GROUPS_PER_KV_LOAD):
-            load_weight_words(nc, k_words, w_qkv_tern_words, g, GROUPS_PER_KV_LOAD, Q_COLS)
-        for g in range(0, GROUPS, GROUPS_PER_KV_LOAD):
-            load_weight_words(nc, v_words, w_qkv_tern_words, g, GROUPS_PER_KV_LOAD, Q_COLS + KV_COLS)
+        for i, (first_bank, n_banks) in enumerate(BLOCKS):
+            if i == 0:
+                load_block_scales(nc.sync, w_planes[i][:], w_qkv_tern_scales, I32, first_bank, n_banks)
+            else:
+                load_block_scales(nc.gpsimd, w_planes[i][:], w_qkv_tern_scales, F32, first_bank, n_banks)
+        nc.sync.dma_start(out=gain_row[0:1, 0:Q_HEADS], in_=q_gain.unsqueeze(0))
+        for i, (first_bank, n_banks) in enumerate(BLOCKS):
+            load_block_words(nc, w_words[i], w_qkv_tern_words, first_bank, n_banks)
 
         x_words = x_sb[:].bitcast(F32)
         grouped_words = x_grouped[:].bitcast(F32).rearrange("p g (s u) -> p g s u", u=2)
@@ -186,86 +184,77 @@ def tile_causalselfattention_pa_k_kernel(
                 in_=x_grouped[:, some, :].rearrange("p g c -> p (g c)"),
             )
 
-        table = build_rotation_table(nc, keep)
+        table = build_rotation_table(nc, keep, token_i)
         sin_j = table[:, 0, :].unsqueeze(1).to_broadcast([P, HEADS_PER_BANK, HALF])
         cos_j = table[:, 1, :].unsqueeze(1).unsqueeze(1).to_broadcast([P, HEADS_PER_BANK, 2, HALF])
         minus_sin_j = table[:, 2, :].unsqueeze(1).to_broadcast([P, HEADS_PER_BANK, HALF])
         gain_ps = psum_x.tile([P, GAIN_PAD], F32, tag="x_t")
         nc.tensor.matmul(out=gain_ps[:], lhsT=ones[:], rhs=gain_row[:], start=True, stop=True)
-        nc.vector.tensor_copy(out=gain[:], in_=gain_ps[:, 0 : Q_COLS // HEAD])
+        nc.vector.tensor_copy(out=gain[:], in_=gain_ps[:, 0:Q_HEADS])
         nc.vector.memset(eps[:], RMS_EPS)
 
         acc = [psum_acc.tile([P, BANK], F32, name="acc%d" % b) for b in range(N_BANKS)]
-        root = [keep.tile([P, HEADS_PER_BANK], F32, name="root%d" % b) for b in range(K_BANK + 1)]
-        factor = [keep.tile([P, HEADS_PER_BANK], F32, name="factor%d" % b) for b in range(K_BANK + 1)]
 
-        def multiply(g, b, bank_words):
-            nc.tensor.matmul_mx(
-                out=acc[b][:],
-                lhsT=x_codes[:, g, :].bitcast(FP8X4),
-                lhsT_scale=x_planes[:, g, :],
-                rhs=bank_words.bitcast(FP4X4),
-                rhs_scale=w_planes[g // SCALE_CHUNK][:, g % SCALE_CHUNK, BANK * b : BANK * (b + 1)],
-                start=(g == 0),
-                stop=(g == GROUPS - 1),
-            )
-
-        def root_mean_square(b):
-            squares = work.tile([P, BANK], F32)
-            sum_sq = work.tile([P, HEADS_PER_BANK], F32)
-            for h in range(HEADS_PER_BANK):
-                cols = slice(h * HEAD, (h + 1) * HEAD)
-                nc.scalar.activation(
-                    out=squares[:, cols],
-                    in_=acc[b][:, cols],
-                    func=ACT.Square,
-                    accum_out=sum_sq[:, h : h + 1],
-                )
+        def norm_and_rotate(first_bank, n_banks):
+            heads = n_banks * HEADS_PER_BANK
+            first_head = first_bank * HEADS_PER_BANK
+            block = staged[:, BANK * first_bank : BANK * (first_bank + n_banks)]
+            sum_sq = work.tile([P, heads], F32, tag="sum_sq")
+            root = work.tile([P, heads], F32, tag="root")
+            factor = work.tile([P, heads], F32, tag="factor")
+            cross = work.tile([P, 2, heads, HALF], F32, tag="cross")
+            for i in range(n_banks):
+                squares = work.tile([P, BANK], F32, tag="squares")
+                for h in range(HEADS_PER_BANK):
+                    cols = slice(h * HEAD, (h + 1) * HEAD)
+                    nc.scalar.activation(
+                        out=squares[:, cols],
+                        in_=acc[first_bank + i][:, cols],
+                        func=ACT.Square,
+                        accum_out=sum_sq[:, i * HEADS_PER_BANK + h : i * HEADS_PER_BANK + h + 1],
+                    )
             nc.scalar.activation(
-                out=root[b][:], in_=sum_sq[:], func=ACT.Sqrt, scale=1.0 / HEAD, bias=eps[:, 0:1]
+                out=root[:], in_=sum_sq[:], func=ACT.Sqrt, scale=1.0 / HEAD, bias=eps[:, 0:1]
             )
-
-        def rotate(b):
-            nc.vector.reciprocal(out=factor[b][:], in_=root[b][:])
-            if b < Q_BANKS:
-                heads = slice(b * HEADS_PER_BANK, (b + 1) * HEADS_PER_BANK)
-                nc.vector.tensor_mul(out=factor[b][:], in0=factor[b][:], in1=gain[:, heads])
-            u = acc[b][:].rearrange("p (h two j) -> p h two j", two=2, j=HALF)
-            same = staged[:, BANK * b : BANK * (b + 1)]
-            cross = work.tile([P, HEADS_PER_BANK, 2, HALF], F32)
-            nc.vector.tensor_mul(
-                out=same.rearrange("p (h two j) -> p h two j", two=2, j=HALF), in0=u, in1=cos_j
-            )
-            nc.vector.tensor_mul(out=cross[:, :, 0, :], in0=u[:, :, 1, :], in1=sin_j)
-            nc.vector.tensor_mul(out=cross[:, :, 1, :], in0=u[:, :, 0, :], in1=minus_sin_j)
-            nc.gpsimd.tensor_add(out=same, in0=same, in1=cross[:].rearrange("p h two j -> p (h two j)"))
-
-        def scale_heads(b):
-            for h in range(HEADS_PER_BANK):
-                cols = slice(BANK * b + h * HEAD, BANK * b + (h + 1) * HEAD)
-                nc.scalar.activation(
-                    out=staged[:, cols], in_=staged[:, cols], func=ACT.Copy, scale=factor[b][:, h : h + 1]
+            for i in range(n_banks):
+                u = acc[first_bank + i][:].rearrange("p (h two j) -> p h two j", two=2, j=HALF)
+                own = slice(i * HEADS_PER_BANK, (i + 1) * HEADS_PER_BANK)
+                nc.vector.tensor_mul(
+                    out=block[:, BANK * i : BANK * (i + 1)].rearrange(
+                        "p (h two j) -> p h two j", two=2, j=HALF
+                    ),
+                    in0=u,
+                    in1=cos_j,
                 )
+                nc.vector.tensor_mul(out=cross[:, 0, own, :], in0=u[:, :, 1, :], in1=sin_j)
+                nc.vector.tensor_mul(out=cross[:, 1, own, :], in0=u[:, :, 0, :], in1=minus_sin_j)
+            nc.vector.reciprocal(out=factor[:], in_=root[:])
+            if first_head < Q_HEADS:
+                nc.vector.tensor_mul(
+                    out=factor[:], in0=factor[:], in1=gain[:, first_head : first_head + heads]
+                )
+            halves = block.rearrange("p (h two j) -> p two h j", two=2, j=HALF)
+            nc.vector.tensor_add(out=halves, in0=halves, in1=cross[:])
+            by_head = block.rearrange("p (h d) -> p h d", d=HEAD)
+            nc.vector.tensor_mul(
+                out=by_head, in0=by_head, in1=factor[:].unsqueeze(2).to_broadcast([P, heads, HEAD])
+            )
 
-        def store(rows, b):
-            nc.sync.dma_start(out=rows, in_=staged[:, BANK * b : BANK * (b + 1)])
-
-        for g in range(GROUPS):
-            for b in range(Q_BANKS):
-                multiply(g, b, q_words[:, g, 2 * BANK * b : 2 * BANK * (b + 1)])
-        for g in range(GROUPS):
-            multiply(g, K_BANK, k_words[:, g, :])
-        for g in range(GROUPS):
-            multiply(g, V_BANK, v_words[:, g, :])
-
-        for b in range(K_BANK + 1):
-            root_mean_square(b)
-        for b in range(K_BANK + 1):
-            rotate(b)
-        nc.vector.tensor_copy(out=staged[:, BANK * V_BANK : BANK * (V_BANK + 1)], in_=acc[V_BANK][:])
-        for b in range(Q_BANKS):
-            scale_heads(b)
-            store(q_rows[:, BANK * b : BANK * (b + 1)], b)
-        store(v_rows, V_BANK)
-        scale_heads(K_BANK)
-        store(k_rows, K_BANK)
+        for i, (first_bank, n_banks) in enumerate(BLOCKS):
+            for g in range(GROUPS):
+                for j in range(n_banks):
+                    nc.tensor.matmul_mx(
+                        out=acc[first_bank + j][:],
+                        lhsT=x_codes[:, g, :].bitcast(FP8X4),
+                        lhsT_scale=x_planes[:, g, :],
+                        rhs=w_words[i][:, g, 2 * BANK * j : 2 * BANK * (j + 1)].bitcast(FP4X4),
+                        rhs_scale=w_planes[i][:, g, BANK * j : BANK * (j + 1)],
+                        start=(g == 0),
+                        stop=(g == GROUPS - 1),
+                    )
+            block = staged[:, BANK * first_bank : BANK * (first_bank + n_banks)]
+            if first_bank == V_BANK:
+                nc.vector.tensor_copy(out=block, in_=acc[V_BANK][:])
+            else:
+                norm_and_rotate(first_bank, n_banks)
+            nc.sync.dma_start(out=block_rows[i], in_=block)

@@ -31,6 +31,7 @@ ROPE_BASE = 10000.0
 RMS_EPS = 1.1920929e-07
 
 X_CHUNK_GROUPS = 4
+SCALE_CHUNK = 4
 PASSES_PER_LOAD = 4
 GAIN_PAD = 32
 
@@ -42,11 +43,15 @@ TWO_PI_LOW = 2.0 * math.pi - TWO_PI_HIGH - TWO_PI_MID
 FLOPS = 2 * P * DIM * N_BANKS * BANK
 
 
-def load_block_scales(queue, planes, scales, word, first_bank, n_banks):
-    some = slice(first_bank * BANK // 4, (first_bank + n_banks) * BANK // 4)
-    by_row = scales.bitcast(word).rearrange("g (quadrant row) n -> row quadrant g n", row=4)
-    for row in range(4):
-        queue.dma_start(out=planes.bitcast(word)[row:P:32, :, :], in_=by_row[row, :, :, some])
+def load_weight_scales(nc, planes, scales, first_group):
+    some = slice(first_group, first_group + SCALE_CHUNK)
+    by_row = scales.bitcast(I32).rearrange("g (quadrant row) n -> row quadrant g n", row=4)
+    for quadrant in range(2):
+        for row in range(4):
+            nc.sync.dma_start(
+                out=planes.bitcast(I32)[32 * quadrant + row : P : 64, :, :],
+                in_=by_row[row, quadrant:4:2, some, :],
+            )
 
 
 def load_block_words(nc, block_words, words, first_bank, n_banks):
@@ -127,8 +132,8 @@ def tile_causalselfattention_pa_k_kernel(
             for first, n in BLOCKS
         ]
         w_planes = [
-            keep.tile([P, GROUPS, BANK * n], U8, align_bytes=64, name="w_planes%d" % first)
-            for first, n in BLOCKS
+            keep.tile([P, SCALE_CHUNK, N_BANKS * BANK], U8, align_bytes=64, name="w_planes%d" % c)
+            for c in range(GROUPS // SCALE_CHUNK)
         ]
         gain_row = keep.tile([P, GAIN_PAD], BF16)
         ones = keep.tile([P, P], BF16)
@@ -150,12 +155,9 @@ def tile_causalselfattention_pa_k_kernel(
             nc.sync.dma_start(
                 out=x_sb[:, first : first + x_chunk], in_=x_rows[:, first : first + x_chunk]
             )
-        for i, (first_bank, n_banks) in enumerate(BLOCKS):
-            if i == 0:
-                load_block_scales(nc.sync, w_planes[i][:], w_qkv_tern_scales, I32, first_bank, n_banks)
-            else:
-                load_block_scales(nc.gpsimd, w_planes[i][:], w_qkv_tern_scales, F32, first_bank, n_banks)
         nc.sync.dma_start(out=gain_row[0:1, 0:Q_HEADS], in_=q_gain.unsqueeze(0))
+        for c in range(GROUPS // SCALE_CHUNK):
+            load_weight_scales(nc, w_planes[c][:], w_qkv_tern_scales, c * SCALE_CHUNK)
         for i, (first_bank, n_banks) in enumerate(BLOCKS):
             load_block_words(nc, w_words[i], w_qkv_tern_words, first_bank, n_banks)
 
@@ -248,7 +250,9 @@ def tile_causalselfattention_pa_k_kernel(
                         lhsT=x_codes[:, g, :].bitcast(FP8X4),
                         lhsT_scale=x_planes[:, g, :],
                         rhs=w_words[i][:, g, 2 * BANK * j : 2 * BANK * (j + 1)].bitcast(FP4X4),
-                        rhs_scale=w_planes[i][:, g, BANK * j : BANK * (j + 1)],
+                        rhs_scale=w_planes[g // SCALE_CHUNK][
+                            :, g % SCALE_CHUNK, BANK * (first_bank + j) : BANK * (first_bank + j + 1)
+                        ],
                         start=(g == 0),
                         stop=(g == GROUPS - 1),
                     )

@@ -33,6 +33,7 @@ RMS_EPS = 1.1920929e-07
 X_CHUNK_GROUPS = 4
 SCALE_CHUNK = 4
 PASSES_PER_LOAD = 4
+LAST_LOADS = (2, 1, 1)
 GAIN_PAD = 32
 
 ROUND_MAGIC = 12582912.0
@@ -57,12 +58,17 @@ def load_weight_scales(nc, planes, scales, first_group):
 def load_block_words(nc, block_words, words, first_bank, n_banks):
     some = slice(2 * BANK * first_bank, 2 * BANK * (first_bank + n_banks))
     groups_per_load = PASSES_PER_LOAD // n_banks
-    for first in range(0, GROUPS, groups_per_load):
-        groups = slice(first, first + groups_per_load)
+    sizes = [groups_per_load] * (GROUPS // groups_per_load)
+    if first_bank == V_BANK:
+        sizes = sizes[:-1] + list(LAST_LOADS)
+    first = 0
+    for size in sizes:
+        groups = slice(first, first + size)
         nc.sync.dma_start(
             out=block_words[:, groups, :].bitcast(I32),
             in_=words[groups, :, some].bitcast(I32).rearrange("g p c -> p g c"),
         )
+        first += size
 
 
 def build_rotation_table(nc, pool, token_i):

@@ -32,8 +32,8 @@ RMS_EPS = 1.1920929e-07
 
 X_CHUNK_GROUPS = 4
 SCALE_CHUNK = 4
-PASSES_PER_LOAD = 4
-LAST_LOADS = (2, 1, 1)
+PASSES_PER_LOAD = 8
+LAST_LOADS = (4, 2, 1, 1)
 GAIN_PAD = 32
 
 ROUND_MAGIC = 12582912.0
@@ -156,12 +156,8 @@ def tile_causalselfattention_pa_k_kernel(
             nc.vector.memset(planes[:].bitcast(I32), 0)
         nc.vector.memset(gain_row[:], 0.0)
         nc.vector.memset(ones[:], 1.0)
-        x_chunk = X_CHUNK_GROUPS * K_GROUP
-        for first in range(0, DIM, x_chunk):
-            nc.sync.dma_start(
-                out=x_sb[:, first : first + x_chunk], in_=x_rows[:, first : first + x_chunk]
-            )
-        nc.sync.dma_start(out=gain_row[0:1, 0:Q_HEADS], in_=q_gain.unsqueeze(0))
+        nc.sync.dma_start(out=x_sb[:], in_=x_rows)
+        nc.scalar.dma_start(out=gain_row[0:1, 0:Q_HEADS], in_=q_gain.unsqueeze(0))
         for c in range(GROUPS // SCALE_CHUNK):
             load_weight_scales(nc, w_planes[c][:], w_qkv_tern_scales, c * SCALE_CHUNK)
         for i, (first_bank, n_banks) in enumerate(BLOCKS):

@@ -152,16 +152,17 @@ def tile_causalselfattention_pa_k_kernel(
         make_identity(nc, identity[:])
         nc.gpsimd.iota(token_i[:], pattern=[[0, 1]], base=0, channel_multiplier=1)
 
+        nc.vector.memset(gain_row[:], 0.0)
         for planes in w_planes:
             nc.vector.memset(planes[:].bitcast(I32), 0)
-        nc.vector.memset(gain_row[:], 0.0)
         nc.vector.memset(ones[:], 1.0)
         nc.sync.dma_start(out=x_sb[:], in_=x_rows)
         nc.scalar.dma_start(out=gain_row[0:1, 0:Q_HEADS], in_=q_gain.unsqueeze(0))
-        for c in range(GROUPS // SCALE_CHUNK):
-            load_weight_scales(nc, w_planes[c][:], w_qkv_tern_scales, c * SCALE_CHUNK)
         for i, (first_bank, n_banks) in enumerate(BLOCKS):
             load_block_words(nc, w_words[i], w_qkv_tern_words, first_bank, n_banks)
+            if i == 0:
+                for c in range(GROUPS // SCALE_CHUNK):
+                    load_weight_scales(nc, w_planes[c][:], w_qkv_tern_scales, c * SCALE_CHUNK)
 
         x_words = x_sb[:].bitcast(F32)
         grouped_words = x_grouped[:].bitcast(F32).rearrange("p g (s u) -> p g s u", u=2)

import math
from contextlib import ExitStack

import concourse.mybir as mybir
from concourse.masks import make_identity

F32 = mybir.dt.float32
BF16 = mybir.dt.bfloat16
I32 = mybir.dt.int32
U32 = mybir.dt.uint32
U8 = mybir.dt.uint8
FP8X4 = mybir.dt.float8_e4m3fn_x4
FP4X4 = mybir.dt.float4_e2m1fn_x4
ALU = mybir.AluOpType
ACT = mybir.ActivationFunctionType

P = 128
PACK = 4
K_GROUP = P * PACK
DIM = 8192
GROUPS = DIM // K_GROUP
HEAD = 128
HALF = HEAD // 2
BANK = 512
HEADS_PER_BANK = BANK // HEAD
Q_HEADS = 16
N_BANKS = 6
V_BANK = 5
BLOCKS = ((0, 2), (2, 2), (4, 1), (V_BANK, 1))
ROPE_BASE = 10000.0
RMS_EPS = 1.1920929e-07

X_CHUNK_GROUPS = 4
SCALE_CHUNK = 4
PASSES_PER_LOAD = 8
LAST_LOADS = (4, 2, 1, 1)
GAIN_PAD = 32

ROUND_MAGIC = 12582912.0
TWO_PI_HIGH = 6.28125
TWO_PI_MID = 0.0019350051879882812
TWO_PI_LOW = 2.0 * math.pi - TWO_PI_HIGH - TWO_PI_MID

FLOPS = 2 * P * DIM * N_BANKS * BANK


def load_weight_scales(nc, planes, scales, first_group):
    some = slice(first_group, first_group + SCALE_CHUNK)
    by_row = scales.bitcast(I32).rearrange("g (quadrant row) n -> row quadrant g n", row=4)
    for quadrant in range(2):
        for row in range(4):
            nc.sync.dma_start(
                out=planes.bitcast(I32)[32 * quadrant + row : P : 64, :, :],
                in_=by_row[row, quadrant:4:2, some, :],
            )


def load_block_words(nc, block_words, words, first_bank, n_banks):
    some = slice(2 * BANK * first_bank, 2 * BANK * (first_bank + n_banks))
    groups_per_load = PASSES_PER_LOAD // n_banks
    sizes = [groups_per_load] * (GROUPS // groups_per_load)
    if first_bank == V_BANK:
        sizes = sizes[:-1] + list(LAST_LOADS)
    first = 0
    for size in sizes:
        groups = slice(first, first + size)
        nc.sync.dma_start(
            out=block_words[:, groups, :].bitcast(I32),
            in_=words[groups, :, some].bitcast(I32).rearrange("g p c -> p g c"),
        )
        first += size


def build_rotation_table(nc, pool, token_i):
    token = pool.tile([P, 1], F32)
    nc.vector.tensor_copy(out=token[:], in_=token_i[:])

    inv_freq = pool.tile([P, HALF], F32)
    nc.vector.memset(inv_freq[:], 1.0)
    for step in (1, 2, 4, 8, 16, 32):
        bit_set = inv_freq[:].rearrange("p (a b c) -> p a b c", b=2, c=step)[:, :, 1, :]
        nc.vector.tensor_scalar_mul(out=bit_set, in0=bit_set, scalar1=ROPE_BASE ** (-step / HALF))

    angle = pool.tile([P, 2, HALF], F32)
    nc.vector.tensor_scalar_mul(out=angle[:, 0, :], in0=inv_freq[:], scalar1=token[:, 0:1])
    nc.vector.tensor_scalar(
        out=angle[:, 1, :],
        in0=inv_freq[:],
        scalar1=token[:, 0:1],
        scalar2=math.pi / 2.0,
        op0=ALU.mult,
        op1=ALU.add,
    )
    flat_angle = angle[:].rearrange("p a j -> p (a j)")
    turns = pool.tile([P, 2 * HALF], F32)
    nc.vector.tensor_scalar(
        out=turns[:],
        in0=flat_angle,
        scalar1=1.0 / (2.0 * math.pi),
        scalar2=ROUND_MAGIC,
        op0=ALU.mult,
        op1=ALU.add,
    )
    nc.vector.tensor_single_scalar(out=turns[:], in_=turns[:], scalar=ROUND_MAGIC, op=ALU.subtract)
    for part in (TWO_PI_HIGH, TWO_PI_MID, TWO_PI_LOW):
        nc.vector.scalar_tensor_tensor(
            out=flat_angle, in0=turns[:], scalar=-part, in1=flat_angle, op0=ALU.mult, op1=ALU.add
        )
    table = pool.tile([P, 3, HALF], F32)
    nc.scalar.activation(out=table[:, 0:2, :], in_=angle[:], func=ACT.Sin)
    nc.vector.tensor_scalar_mul(out=table[:, 2, :], in0=table[:, 0, :], scalar1=-1.0)
    return table


def tile_causalselfattention_pa_k_kernel(
    tc, x, w_qkv_tern_words, w_qkv_tern_scales, q_gain, out_0, out_1, out_2
):
    nc = tc.nc
    x_rows = x.flatten_outer_dims()
    q_rows = out_0.rearrange("b s h d -> (b s) (h d)")
    k_rows = out_1.rearrange("b s h d -> (b s) (h d)")
    v_rows = out_2.rearrange("b s h d -> (b s) (h d)")
    block_rows = (q_rows[:, 0 : 2 * BANK], q_rows[:, 2 * BANK : 4 * BANK], k_rows, v_rows)

    with ExitStack() as ctx:
        ctx.enter_context(tc.manual_schedule())
        keep = ctx.enter_context(tc.tile_pool(name="keep", bufs=1))
        work = ctx.enter_context(tc.tile_pool(name="work", bufs=2))
        psum_x = ctx.enter_context(tc.psum_pool(name="psum_x", bufs=2))
        psum_acc = ctx.enter_context(tc.psum_pool(name="psum_acc", bufs=1))

        x_sb = keep.tile([P, DIM], BF16)
        x_grouped = keep.tile([P, GROUPS, P * PACK], BF16, align_bytes=64)
        x_codes = keep.tile([P, GROUPS, P], U32, align_bytes=64)
        x_planes = keep.tile([P, GROUPS, P], U8, align_bytes=64)
        w_words = [
            keep.tile([P, GROUPS, 2 * BANK * n], U8, align_bytes=64, name="w_words%d" % first)
            for first, n in BLOCKS
        ]
        w_planes = [
            keep.tile([P, SCALE_CHUNK, N_BANKS * BANK], U8, align_bytes=64, name="w_planes%d" % c)
            for c in range(GROUPS // SCALE_CHUNK)
        ]
        gain_row = keep.tile([P, GAIN_PAD], BF16)
        ones = keep.tile([P, P], BF16)
        gain = keep.tile([P, Q_HEADS], F32)
        eps = keep.tile([P, 1], F32)
        identity = keep.tile([P, P], F32)
        token_i = keep.tile([P, 1], I32)
        staged = keep.tile([P, N_BANKS * BANK], F32)

        make_identity(nc, identity[:])
        nc.gpsimd.iota(token_i[:], pattern=[[0, 1]], base=0, channel_multiplier=1)

        nc.vector.memset(gain_row[:], 0.0)
        for planes in w_planes:
            nc.vector.memset(planes[:].bitcast(I32), 0)
        nc.vector.memset(ones[:], 1.0)
        nc.sync.dma_start(out=x_sb[:], in_=x_rows)
        nc.scalar.dma_start(out=gain_row[0:1, 0:Q_HEADS], in_=q_gain.unsqueeze(0))
        for i, (first_bank, n_banks) in enumerate(BLOCKS):
            load_block_words(nc, w_words[i], w_qkv_tern_words, first_bank, n_banks)
            if i == 0:
                for c in range(GROUPS // SCALE_CHUNK):
                    load_weight_scales(nc, w_planes[c][:], w_qkv_tern_scales, c * SCALE_CHUNK)

        x_words = x_sb[:].bitcast(F32)
        grouped_words = x_grouped[:].bitcast(F32).rearrange("p g (s u) -> p g s u", u=2)
        words_per_group = K_GROUP // 2
        for first_group in range(0, GROUPS, X_CHUNK_GROUPS):
            for pair in range(first_group, first_group + X_CHUNK_GROUPS, 2):
                x_t = psum_x.tile([P, 2, 2, P], F32)
                for i in range(2):
                    start_word = (pair + i) * words_per_group
                    for u in range(2):
                        nc.tensor.transpose(
                            x_t[:, i, u, :],
                            x_words[:, start_word + u : start_word + words_per_group : 2],
                            identity[:],
                        )
                nc.scalar.copy(
                    out=grouped_words[:, pair : pair + 2, :, :],
                    in_=x_t[:].rearrange("p i u s -> p i s u"),
                )
            some = slice(first_group, first_group + X_CHUNK_GROUPS)
            nc.vector.quantize_mx(
                out=x_codes[:, some, :].rearrange("p g s -> p (g s)").bitcast(FP8X4),
                scales=x_planes[:, some, :].rearrange("p g s -> p (g s)"),
                in_=x_grouped[:, some, :].rearrange("p g c -> p (g c)"),
            )

        table = build_rotation_table(nc, keep, token_i)
        sin_j = table[:, 0, :].unsqueeze(1).to_broadcast([P, HEADS_PER_BANK, HALF])
        cos_j = table[:, 1, :].unsqueeze(1).unsqueeze(1).to_broadcast([P, HEADS_PER_BANK, 2, HALF])
        minus_sin_j = table[:, 2, :].unsqueeze(1).to_broadcast([P, HEADS_PER_BANK, HALF])
        gain_ps = psum_x.tile([P, GAIN_PAD], F32, tag="x_t")
        nc.tensor.matmul(out=gain_ps[:], lhsT=ones[:], rhs=gain_row[:], start=True, stop=True)
        nc.vector.tensor_copy(out=gain[:], in_=gain_ps[:, 0:Q_HEADS])
        nc.vector.memset(eps[:], RMS_EPS)

        acc = [psum_acc.tile([P, BANK], F32, name="acc%d" % b) for b in range(N_BANKS)]

        def norm_and_rotate(first_bank, n_banks):
            heads = n_banks * HEADS_PER_BANK
            first_head = first_bank * HEADS_PER_BANK
            block = staged[:, BANK * first_bank : BANK * (first_bank + n_banks)]
            sum_sq = work.tile([P, heads], F32, tag="sum_sq")
            root = work.tile([P, heads], F32, tag="root")
            factor = work.tile([P, heads], F32, tag="factor")
            cross = work.tile([P, 2, heads, HALF], F32, tag="cross")
            for i in range(n_banks):
                squares = work.tile([P, BANK], F32, tag="squares")
                for h in range(HEADS_PER_BANK):
                    cols = slice(h * HEAD, (h + 1) * HEAD)
                    nc.scalar.activation(
                        out=squares[:, cols],
                        in_=acc[first_bank + i][:, cols],
                        func=ACT.Square,
                        accum_out=sum_sq[:, i * HEADS_PER_BANK + h : i * HEADS_PER_BANK + h + 1],
                    )
            nc.scalar.activation(
                out=root[:], in_=sum_sq[:], func=ACT.Sqrt, scale=1.0 / HEAD, bias=eps[:, 0:1]
            )
            for i in range(n_banks):
                u = acc[first_bank + i][:].rearrange("p (h two j) -> p h two j", two=2, j=HALF)
                own = slice(i * HEADS_PER_BANK, (i + 1) * HEADS_PER_BANK)
                nc.vector.tensor_mul(
                    out=block[:, BANK * i : BANK * (i + 1)].rearrange(
                        "p (h two j) -> p h two j", two=2, j=HALF
                    ),
                    in0=u,
                    in1=cos_j,
                )
                nc.vector.tensor_mul(out=cross[:, 0, own, :], in0=u[:, :, 1, :], in1=sin_j)
                nc.vector.tensor_mul(out=cross[:, 1, own, :], in0=u[:, :, 0, :], in1=minus_sin_j)
            nc.vector.reciprocal(out=factor[:], in_=root[:])
            if first_head < Q_HEADS:
                nc.vector.tensor_mul(
                    out=factor[:], in0=factor[:], in1=gain[:, first_head : first_head + heads]
                )
            halves = block.rearrange("p (h two j) -> p two h j", two=2, j=HALF)
            nc.vector.tensor_add(out=halves, in0=halves, in1=cross[:])
            by_head = block.rearrange("p (h d) -> p h d", d=HEAD)
            nc.vector.tensor_mul(
                out=by_head, in0=by_head, in1=factor[:].unsqueeze(2).to_broadcast([P, heads, HEAD])
            )

        for i, (first_bank, n_banks) in enumerate(BLOCKS):
            for g in range(GROUPS):
                for j in range(n_banks):
                    nc.tensor.matmul_mx(
                        out=acc[first_bank + j][:],
                        lhsT=x_codes[:, g, :].bitcast(FP8X4),
                        lhsT_scale=x_planes[:, g, :],
                        rhs=w_words[i][:, g, 2 * BANK * j : 2 * BANK * (j + 1)].bitcast(FP4X4),
                        rhs_scale=w_planes[g // SCALE_CHUNK][
                            :, g % SCALE_CHUNK, BANK * (first_bank + j) : BANK * (first_bank + j + 1)
                        ],
                        start=(g == 0),
                        stop=(g == GROUPS - 1),
                    )
            block = staged[:, BANK * first_bank : BANK * (first_bank + n_banks)]
            if first_bank == V_BANK:
                nc.vector.tensor_copy(out=block, in_=acc[V_BANK][:])
            else:
                norm_and_rotate(first_bank, n_banks)
            nc.sync.dma_start(out=block_rows[i], in_=block)
